import numpy as np
import ml_dtypes


def mxq(x, axis, fmt="e4m3"):
    dtype, down = {"e4m3": (ml_dtypes.float8_e4m3fn, 7), "e5m2": (ml_dtypes.float8_e5m2, 14)}[fmt]
    v = np.moveaxis(np.asarray(x, np.float32).astype(ml_dtypes.bfloat16).astype(np.float64), axis, -1)
    blocks = v.reshape(v.shape[:-1] + (-1, 32))
    amax = np.abs(blocks).max(-1, keepdims=True)
    byte = np.maximum(np.where(amax > 0, np.frexp(amax)[1] - 1 + 127, 0) - down, 1)
    scale = np.exp2(byte - 127.0)
    codes = (blocks / scale).astype(np.float32).astype(dtype).astype(np.float64)
    return np.moveaxis((codes * scale).reshape(v.shape), -1, axis)


WIDE = False


def mx_kscale(k):
    if not WIDE:
        return np.ones(k)
    levels = np.array([20, -20, 10, -10, 0])
    a = np.random.permutation(np.resize(levels, k // 512 * 4)).reshape(k // 512, 4)
    idx = np.arange(k)
    return np.exp2(a[idx // 512, idx % 128 // 32])


BF16 = ml_dtypes.bfloat16


def bf(x):
    return np.asarray(x, np.float32).astype(BF16)


def f64(x):
    return np.asarray(x).astype(np.float64)


B, T, D, F = 2, 256, 128, 8192
BINS = np.array([-1.5, -1.0, -0.5, 0.0, 0.5, 1.0, 1.5])
NB = BINS.shape[0] + 1
INDEX = 0


def buckets(x):
    y = x[..., INDEX]
    return np.sum(np.where(y[..., None] > BINS, 1.0, 0.0), axis=-1).reshape(B * T)


def setup_inputs():
    u = mx_kscale(F)
    x = np.random.standard_normal((B, T, D))
    W = np.random.standard_normal((NB, D, F)) * 0.5 / np.sqrt(D) / u[None, None, :]
    g = np.random.standard_normal((B, T, F)) * np.exp2(np.random.randint(-12, 1, (B, T, 1))) * 16.0 * u
    y = x[..., INDEX]
    near = np.min(np.abs(y[..., None] - BINS), axis=-1) < 0.01
    x[..., INDEX] = np.where(near, y + 0.03, y)
    return {"x": bf(x), "W": bf(W), "grad_out": bf(g)}


def reference(x, W, grad_out):
    x, W, g = f64(x), f64(W), f64(grad_out)
    memf = buckets(x)
    gq = mxq(g.reshape(B * T, F), 1, "e5m2")
    Wq = mxq(W, 2, "e4m3")
    out = np.zeros((B * T, D))
    for k in range(NB):
        sel = np.where(memf == k, 1.0, 0.0)[:, None]
        out = out + sel * (gq @ Wq[k].T)
    return out.reshape(B, T, D)

@@ -1,0 +1,157 @@
+from contextlib import ExitStack
+
+import concourse.mybir as mybir
+from concourse.masks import make_identity
+
+F32 = mybir.dt.float32
+BF16 = mybir.dt.bfloat16
+U32 = mybir.dt.uint32
+U8 = mybir.dt.uint8
+E5M2_X4 = mybir.dt.float8_e5m2_x4
+E4M3_X4 = mybir.dt.float8_e4m3fn_x4
+ALU = mybir.AluOpType
+
+P = 128
+TOKENS = 512
+D = 128
+F = 8192
+EXPERTS = 8
+BOUNDARIES = (-1.5, -1.0, -0.5, 0.0, 0.5, 1.0, 1.5)
+
+K_PASS = 4 * P
+PASSES = F // K_PASS
+ROW_TILES = 4
+ROUNDS = EXPERTS // ROW_TILES
+CHUNK_PASSES = 2
+CHUNK_F = CHUNK_PASSES * K_PASS
+CHUNKS = F // CHUNK_F
+WORDS = K_PASS // 2
+
+FLOPS = 2 * TOKENS * EXPERTS * D * F
+
+
+def quantise_chunk(nc, pools, identity, rows, fp8_x4, codes, scales):
+    raw = pools["raw"].tile([P, ROW_TILES, CHUNK_F], BF16, name="raw")
+    nc.sync.dma_start(out=raw[:], in_=rows)
+
+    grouped = pools["grouped"].tile([P, CHUNK_PASSES, ROW_TILES, P, 4], BF16, name="grouped", align_bytes=64)
+    for c in range(CHUNK_PASSES):
+        for half in range(ROW_TILES // 2):
+            bank = pools["transposed"].tile([P, 2, 2, P], F32, name="bank")
+            for i in range(2):
+                words = raw[:, 2 * half + i, :].bitcast(F32)
+                for u in range(2):
+                    first = c * WORDS + u * P
+                    nc.tensor.transpose(bank[:, i, u, :], words[:, first : first + P], identity[:])
+            engine_copy = nc.vector.tensor_copy if (c, half) == (1, 0) else nc.scalar.copy
+            engine_copy(
+                out=grouped[:, c, 2 * half : 2 * half + 2, :, :].bitcast(F32),
+                in_=bank[:].rearrange("p i u r -> p i r u"),
+            )
+    for c in range(CHUNK_PASSES):
+        nc.vector.quantize_mx(
+            out=codes[:, c, :].bitcast(fp8_x4),
+            scales=scales[:, c, :],
+            in_=grouped[:, c].rearrange("p t r j -> p (t r j)"),
+        )
+
+
+def tile_dispatchbyvariable_pa_k_kernel(tc, x, W, grad_out, out):
+    nc = tc.nc
+    x_rows = x.flatten_outer_dims().rearrange("(t p) d -> p t d", p=P)
+    g_rows = grad_out.flatten_outer_dims().rearrange("(t p) f -> p t f", p=P)
+    w_rows = W.rearrange("k d f -> d k f")
+    out_tiles = out.flatten_outer_dims().rearrange("(t p) d -> t p d", p=P)
+
+    with ExitStack() as ctx:
+        keep = ctx.enter_context(tc.tile_pool(name="keep", bufs=1))
+        pools = {
+            "raw": ctx.enter_context(tc.tile_pool(name="raw", bufs=8)),
+            "grouped": ctx.enter_context(tc.tile_pool(name="grouped", bufs=3)),
+            "transposed": ctx.enter_context(tc.psum_pool(name="transposed", bufs=4)),
+        }
+        w_pool = ctx.enter_context(tc.tile_pool(name="w_codes", bufs=3))
+        acc_pool = ctx.enter_context(tc.psum_pool(name="acc", bufs=1))
+        ctx.enter_context(tc.manual_schedule())
+
+        identity = keep.tile([P, P], F32, name="identity")
+        make_identity(nc, identity[:])
+
+        x_sb = keep.tile([P, ROW_TILES, D], BF16, name="x_sb")
+        nc.scalar.dma_start(out=x_sb[:], in_=x_rows)
+        y = keep.tile([P, ROW_TILES], F32, name="y")
+        nc.vector.tensor_copy(out=y[:], in_=x_sb[:, :, 0])
+        above = keep.tile([P, EXPERTS + 1, ROW_TILES], F32, name="above")
+        nc.vector.memset(above[:, 0, :], 1.0)
+        nc.vector.memset(above[:, EXPERTS, :], 0.0)
+        for j, boundary in enumerate(BOUNDARIES):
+            nc.vector.tensor_single_scalar(out=above[:, j + 1, :], in_=y[:], scalar=boundary, op=ALU.is_gt)
+        sel = keep.tile([P, EXPERTS, ROW_TILES], F32, name="sel")
+        nc.vector.tensor_sub(out=sel[:], in0=above[:, 0:EXPERTS, :], in1=above[:, 1 : EXPERTS + 1, :])
+
+        g_codes = keep.tile([P, PASSES, TOKENS], U32, name="g_codes", align_bytes=64)
+        g_scales = keep.tile([P, PASSES, TOKENS], U8, name="g_scales", align_bytes=64)
+        result = keep.tile([P, ROW_TILES, D], F32, name="result")
+
+        def multiply(rnd, chunk, acc, w_codes, w_scales):
+            for t in range(ROW_TILES):
+                tokens = slice(t * P, (t + 1) * P)
+                for c in range(CHUNK_PASSES):
+                    k_pass = chunk * CHUNK_PASSES + c
+                    nc.tensor.matmul_mx(
+                        out=acc[t][:],
+                        lhsT=g_codes[:, k_pass, tokens].bitcast(E5M2_X4),
+                        lhsT_scale=g_scales[:, k_pass, tokens],
+                        rhs=w_codes[:, c, :].bitcast(E4M3_X4),
+                        rhs_scale=w_scales[:, c, :],
+                        start=(k_pass == 0),
+                        stop=(k_pass == PASSES - 1),
+                    )
+                if chunk == CHUNKS - 1:
+                    add_selected(rnd, t, acc[t])
+
+        def add_selected(rnd, t, products):
+            for i in range(ROW_TILES):
+                k = rnd * ROW_TILES + i
+                if k == 0:
+                    nc.vector.tensor_scalar(
+                        out=result[:, t, :],
+                        in0=products[:, 0:D],
+                        scalar1=sel[:, 0, t : t + 1],
+                        scalar2=None,
+                        op0=ALU.mult,
+                    )
+                else:
+                    nc.vector.scalar_tensor_tensor(
+                        out=result[:, t, :],
+                        in0=products[:, i * D : (i + 1) * D],
+                        scalar=sel[:, k, t : t + 1],
+                        in1=result[:, t, :],
+                        op0=ALU.mult,
+                        op1=ALU.add,
+                    )
+            if rnd == ROUNDS - 1:
+                nc.sync.dma_start(out=out_tiles[t], in_=result[:, t, :])
+
+        waiting = None
+        for rnd in range(ROUNDS):
+            for chunk in range(CHUNKS):
+                features = slice(chunk * CHUNK_F, (chunk + 1) * CHUNK_F)
+                passes = slice(chunk * CHUNK_PASSES, (chunk + 1) * CHUNK_PASSES)
+                if rnd == 0:
+                    quantise_chunk(
+                        nc, pools, identity, g_rows[:, :, features], E5M2_X4,
+                        g_codes[:, passes, :], g_scales[:, passes, :],
+                    )
+                w_codes = w_pool.tile([P, CHUNK_PASSES, ROW_TILES * D], U32, name="w_codes", align_bytes=64)
+                w_scales = w_pool.tile([P, CHUNK_PASSES, ROW_TILES * D], U8, name="w_scales", align_bytes=64)
+                experts = slice(rnd * ROW_TILES, (rnd + 1) * ROW_TILES)
+                quantise_chunk(
+                    nc, pools, identity, w_rows[:, experts, features], E4M3_X4, w_codes, w_scales
+                )
+                if waiting is not None:
+                    multiply(*waiting)
+                if chunk == 0:
+                    acc = [acc_pool.tile([P, ROW_TILES * D], F32, name="acc%d" % t) for t in range(ROW_TILES)]
+                waiting = (rnd, chunk, acc, w_codes, w_scales)
+        multiply(*waiting)

@@ -93,10 +93,10 @@ def tile_dispatchbyvariable_pa_k_kernel(tc, x, W, grad_out, out):
         g_scales = keep.tile([P, PASSES, TOKENS], U8, name="g_scales", align_bytes=64)
         result = keep.tile([P, ROW_TILES, D], F32, name="result")
 
-        def multiply(rnd, chunk, acc, w_codes, w_scales):
+        def multiply(which, rnd, chunk, acc, w_codes, w_scales):
             for t in range(ROW_TILES):
                 tokens = slice(t * P, (t + 1) * P)
-                for c in range(CHUNK_PASSES):
+                for c in which:
                     k_pass = chunk * CHUNK_PASSES + c
                     nc.tensor.matmul_mx(
                         out=acc[t][:],
@@ -107,7 +107,7 @@ def tile_dispatchbyvariable_pa_k_kernel(tc, x, W, grad_out, out):
                         start=(k_pass == 0),
                         stop=(k_pass == PASSES - 1),
                     )
-                if chunk == CHUNKS - 1:
+                if chunk == CHUNKS - 1 and CHUNK_PASSES - 1 in which:
                     add_selected(rnd, t, acc[t])
 
         def add_selected(rnd, t, products):
@@ -143,6 +143,8 @@ def tile_dispatchbyvariable_pa_k_kernel(tc, x, W, grad_out, out):
                         nc, pools, identity, g_rows[:, :, features], E5M2_X4,
                         g_codes[:, passes, :], g_scales[:, passes, :],
                     )
+                    if waiting is not None:
+                        multiply((0,), *waiting)
                 w_codes = w_pool.tile([P, CHUNK_PASSES, ROW_TILES * D], U32, name="w_codes", align_bytes=64)
                 w_scales = w_pool.tile([P, CHUNK_PASSES, ROW_TILES * D], U8, name="w_scales", align_bytes=64)
                 experts = slice(rnd * ROW_TILES, (rnd + 1) * ROW_TILES)
@@ -150,8 +152,8 @@ def tile_dispatchbyvariable_pa_k_kernel(tc, x, W, grad_out, out):
                     nc, pools, identity, w_rows[:, experts, features], E4M3_X4, w_codes, w_scales
                 )
                 if waiting is not None:
-                    multiply(*waiting)
+                    multiply((1,) if rnd == 0 else (0, 1), *waiting)
                 if chunk == 0:
                     acc = [acc_pool.tile([P, ROW_TILES * D], F32, name="acc%d" % t) for t in range(ROW_TILES)]
                 waiting = (rnd, chunk, acc, w_codes, w_scales)
-        multiply(*waiting)
+        multiply((0, 1), *waiting)

@@ -20,38 +20,43 @@ BOUNDARIES = (-1.5, -1.0, -0.5, 0.0, 0.5, 1.0, 1.5)
 
 K_PASS = 4 * P
 PASSES = F // K_PASS
-ROW_TILES = 4
-ROUNDS = EXPERTS // ROW_TILES
-CHUNK_PASSES = 2
-CHUNK_F = CHUNK_PASSES * K_PASS
-CHUNKS = F // CHUNK_F
 WORDS = K_PASS // 2
+ROW_TILES = 4
+ROWS = ROW_TILES * P
+
+CHUNK_PASSES = 2
+EVEN_CHUNKS = [(c, CHUNK_PASSES) for c in range(0, PASSES, CHUNK_PASSES)]
+TAPERED_CHUNKS = [(0, 1), (1, 1)] + EVEN_CHUNKS[1:]
 
 FLOPS = 2 * TOKENS * EXPERTS * D * F
 
 
-def quantise_chunk(nc, pools, identity, rows, fp8_x4, codes, scales):
-    raw = pools["raw"].tile([P, ROW_TILES, CHUNK_F], BF16, name="raw")
-    nc.sync.dma_start(out=raw[:], in_=rows)
-
+def quantise_chunk(nc, pools, identity, rows, chunk, fp8_x4, codes, scales):
+    first_pass, n_passes = chunk
     grouped = pools["grouped"].tile([P, CHUNK_PASSES, ROW_TILES, P, 4], BF16, name="grouped", align_bytes=64)
-    for c in range(CHUNK_PASSES):
-        for half in range(ROW_TILES // 2):
+    for half in range(ROW_TILES // 2):
+        tiles = slice(2 * half, 2 * half + 2)
+        raw = pools["raw"].tile([P, 2, CHUNK_PASSES * K_PASS], BF16, name="raw")
+        nc.sync.dma_start(
+            out=raw[:, :, 0 : n_passes * K_PASS],
+            in_=rows[:, tiles, first_pass * K_PASS : (first_pass + n_passes) * K_PASS],
+        )
+        for c in range(n_passes):
             bank = pools["transposed"].tile([P, 2, 2, P], F32, name="bank")
             for i in range(2):
-                words = raw[:, 2 * half + i, :].bitcast(F32)
+                words = raw[:, i, :].bitcast(F32)
                 for u in range(2):
-                    first = c * WORDS + u * P
-                    nc.tensor.transpose(bank[:, i, u, :], words[:, first : first + P], identity[:])
-            engine_copy = nc.vector.tensor_copy if (c, half) == (1, 0) else nc.scalar.copy
-            engine_copy(
-                out=grouped[:, c, 2 * half : 2 * half + 2, :, :].bitcast(F32),
+                    start = c * WORDS + u * P
+                    nc.tensor.transpose(bank[:, i, u, :], words[:, start : start + P], identity[:])
+            copy_out = nc.vector.tensor_copy if (half, c) == (0, 1) else nc.scalar.copy
+            copy_out(
+                out=grouped[:, c, tiles, :, :].bitcast(F32),
                 in_=bank[:].rearrange("p i u r -> p i r u"),
             )
-    for c in range(CHUNK_PASSES):
+    for c in range(n_passes):
         nc.vector.quantize_mx(
-            out=codes[:, c, :].bitcast(fp8_x4),
-            scales=scales[:, c, :],
+            out=codes[:, first_pass + c, :].bitcast(fp8_x4),
+            scales=scales[:, first_pass + c, :],
             in_=grouped[:, c].rearrange("p t r j -> p (t r j)"),
         )
 
@@ -66,11 +71,10 @@ def tile_dispatchbyvariable_pa_k_kernel(tc, x, W, grad_out, out):
     with ExitStack() as ctx:
         keep = ctx.enter_context(tc.tile_pool(name="keep", bufs=1))
         pools = {
-            "raw": ctx.enter_context(tc.tile_pool(name="raw", bufs=8)),
+            "raw": ctx.enter_context(tc.tile_pool(name="raw", bufs=12)),
             "grouped": ctx.enter_context(tc.tile_pool(name="grouped", bufs=3)),
             "transposed": ctx.enter_context(tc.psum_pool(name="transposed", bufs=4)),
         }
-        w_pool = ctx.enter_context(tc.tile_pool(name="w_codes", bufs=3))
         acc_pool = ctx.enter_context(tc.psum_pool(name="acc", bufs=1))
         ctx.enter_context(tc.manual_schedule())
 
@@ -80,43 +84,48 @@ def tile_dispatchbyvariable_pa_k_kernel(tc, x, W, grad_out, out):
         x_sb = keep.tile([P, ROW_TILES, D], BF16, name="x_sb")
         nc.scalar.dma_start(out=x_sb[:], in_=x_rows)
         y = keep.tile([P, ROW_TILES], F32, name="y")
-        nc.vector.tensor_copy(out=y[:], in_=x_sb[:, :, 0])
+        nc.gpsimd.tensor_copy(out=y[:], in_=x_sb[:, :, 0])
         above = keep.tile([P, EXPERTS + 1, ROW_TILES], F32, name="above")
-        nc.vector.memset(above[:, 0, :], 1.0)
-        nc.vector.memset(above[:, EXPERTS, :], 0.0)
+        nc.gpsimd.memset(above[:, 0, :], 1.0)
+        nc.gpsimd.memset(above[:, EXPERTS, :], 0.0)
         for j, boundary in enumerate(BOUNDARIES):
-            nc.vector.tensor_single_scalar(out=above[:, j + 1, :], in_=y[:], scalar=boundary, op=ALU.is_gt)
+            nc.gpsimd.tensor_single_scalar(out=above[:, j + 1, :], in_=y[:], scalar=boundary, op=ALU.is_gt)
         sel = keep.tile([P, EXPERTS, ROW_TILES], F32, name="sel")
-        nc.vector.tensor_sub(out=sel[:], in0=above[:, 0:EXPERTS, :], in1=above[:, 1 : EXPERTS + 1, :])
+        nc.gpsimd.tensor_tensor(
+            out=sel[:], in0=above[:, 0:EXPERTS, :], in1=above[:, 1 : EXPERTS + 1, :], op=ALU.subtract
+        )
 
-        g_codes = keep.tile([P, PASSES, TOKENS], U32, name="g_codes", align_bytes=64)
-        g_scales = keep.tile([P, PASSES, TOKENS], U8, name="g_scales", align_bytes=64)
+        g_codes = keep.tile([P, PASSES, ROWS], U32, name="g_codes", align_bytes=64)
+        g_scales = keep.tile([P, PASSES, ROWS], U8, name="g_scales", align_bytes=64)
+        w_codes = [keep.tile([P, PASSES, ROWS], U32, name="w_codes%d" % group, align_bytes=64) for group in range(2)]
+        w_scales = [keep.tile([P, PASSES, ROWS], U8, name="w_scales%d" % group, align_bytes=64) for group in range(2)]
         result = keep.tile([P, ROW_TILES, D], F32, name="result")
+        acc = {}
 
-        def multiply(which, rnd, chunk, acc, w_codes, w_scales):
-            for t in range(ROW_TILES):
+        def multiply(todo):
+            for group, c, t in todo:
+                if c == 0:
+                    acc[t] = acc_pool.tile([P, ROWS], F32, name="acc%d" % t)
                 tokens = slice(t * P, (t + 1) * P)
-                for c in which:
-                    k_pass = chunk * CHUNK_PASSES + c
-                    nc.tensor.matmul_mx(
-                        out=acc[t][:],
-                        lhsT=g_codes[:, k_pass, tokens].bitcast(E5M2_X4),
-                        lhsT_scale=g_scales[:, k_pass, tokens],
-                        rhs=w_codes[:, c, :].bitcast(E4M3_X4),
-                        rhs_scale=w_scales[:, c, :],
-                        start=(k_pass == 0),
-                        stop=(k_pass == PASSES - 1),
-                    )
-                if chunk == CHUNKS - 1 and CHUNK_PASSES - 1 in which:
-                    add_selected(rnd, t, acc[t])
+                nc.tensor.matmul_mx(
+                    out=acc[t][:],
+                    lhsT=g_codes[:, c, tokens].bitcast(E5M2_X4),
+                    lhsT_scale=g_scales[:, c, tokens],
+                    rhs=w_codes[group][:, c, :].bitcast(E4M3_X4),
+                    rhs_scale=w_scales[group][:, c, :],
+                    start=(c == 0),
+                    stop=(c == PASSES - 1),
+                )
+                if c == PASSES - 1:
+                    add_selected(group, t)
 
-        def add_selected(rnd, t, products):
+        def add_selected(group, t):
             for i in range(ROW_TILES):
-                k = rnd * ROW_TILES + i
+                k = group * ROW_TILES + i
                 if k == 0:
                     nc.vector.tensor_scalar(
                         out=result[:, t, :],
-                        in0=products[:, 0:D],
+                        in0=acc[t][:, 0:D],
                         scalar1=sel[:, 0, t : t + 1],
                         scalar2=None,
                         op0=ALU.mult,
@@ -124,36 +133,26 @@ def tile_dispatchbyvariable_pa_k_kernel(tc, x, W, grad_out, out):
                 else:
                     nc.vector.scalar_tensor_tensor(
                         out=result[:, t, :],
-                        in0=products[:, i * D : (i + 1) * D],
+                        in0=acc[t][:, i * D : (i + 1) * D],
                         scalar=sel[:, k, t : t + 1],
                         in1=result[:, t, :],
                         op0=ALU.mult,
                         op1=ALU.add,
                     )
-            if rnd == ROUNDS - 1:
+            if k == EXPERTS - 1:
                 nc.sync.dma_start(out=out_tiles[t], in_=result[:, t, :])
 
-        waiting = None
-        for rnd in range(ROUNDS):
-            for chunk in range(CHUNKS):
-                features = slice(chunk * CHUNK_F, (chunk + 1) * CHUNK_F)
-                passes = slice(chunk * CHUNK_PASSES, (chunk + 1) * CHUNK_PASSES)
-                if rnd == 0:
-                    quantise_chunk(
-                        nc, pools, identity, g_rows[:, :, features], E5M2_X4,
-                        g_codes[:, passes, :], g_scales[:, passes, :],
-                    )
-                    if waiting is not None:
-                        multiply((0,), *waiting)
-                w_codes = w_pool.tile([P, CHUNK_PASSES, ROW_TILES * D], U32, name="w_codes", align_bytes=64)
-                w_scales = w_pool.tile([P, CHUNK_PASSES, ROW_TILES * D], U8, name="w_scales", align_bytes=64)
-                experts = slice(rnd * ROW_TILES, (rnd + 1) * ROW_TILES)
-                quantise_chunk(
-                    nc, pools, identity, w_rows[:, experts, features], E4M3_X4, w_codes, w_scales
-                )
-                if waiting is not None:
-                    multiply((1,) if rnd == 0 else (0, 1), *waiting)
-                if chunk == 0:
-                    acc = [acc_pool.tile([P, ROW_TILES * D], F32, name="acc%d" % t) for t in range(ROW_TILES)]
-                waiting = (rnd, chunk, acc, w_codes, w_scales)
-        multiply((0, 1), *waiting)
+        late = []
+        for chunk in TAPERED_CHUNKS:
+            quantise_chunk(nc, pools, identity, g_rows, chunk, E5M2_X4, g_codes, g_scales)
+            multiply(late[: len(late) // 2])
+            quantise_chunk(nc, pools, identity, w_rows[:, 0:ROW_TILES, :], chunk, E4M3_X4, w_codes[0], w_scales[0])
+            multiply(late[len(late) // 2 :])
+            late = [(0, c, t) for c in range(chunk[0], chunk[0] + chunk[1]) for t in range(ROW_TILES)]
+        for chunk in EVEN_CHUNKS:
+            quantise_chunk(nc, pools, identity, w_rows[:, ROW_TILES:EXPERTS, :], chunk, E4M3_X4, w_codes[1], w_scales[1])
+            multiply(late)
+            late = [(1, c, t) for c in range(chunk[0], chunk[0] + chunk[1]) for t in (0, 1)]
+        multiply(late)
+        for t in (2, 3):
+            multiply([(1, c, t) for c in range(PASSES)])

@@ -28,6 +28,8 @@ CHUNK_PASSES = 2
 EVEN_CHUNKS = [(c, CHUNK_PASSES) for c in range(0, PASSES, CHUNK_PASSES)]
 TAPERED_CHUNKS = [(0, 1), (1, 1)] + EVEN_CHUNKS[1:]
 
+RUN_PASSES = 4
+
 FLOPS = 2 * TOKENS * EXPERTS * D * F
 
 
@@ -101,6 +103,7 @@ def tile_dispatchbyvariable_pa_k_kernel(tc, x, W, grad_out, out):
         w_scales = [keep.tile([P, PASSES, ROWS], U8, name="w_scales%d" % group, align_bytes=64) for group in range(2)]
         result = keep.tile([P, ROW_TILES, D], F32, name="result")
         acc = {}
+        closed = []
 
         def multiply(todo):
             for group, c, t in todo:
@@ -117,7 +120,12 @@ def tile_dispatchbyvariable_pa_k_kernel(tc, x, W, grad_out, out):
                     stop=(c == PASSES - 1),
                 )
                 if c == PASSES - 1:
-                    add_selected(group, t)
+                    closed.append((group, t))
+
+        def select(count):
+            for n in range(min(count, len(closed))):
+                group, t = closed.pop(0)
+                add_selected(group, t)
 
         def add_selected(group, t):
             for i in range(ROW_TILES):
@@ -148,11 +156,14 @@ def tile_dispatchbyvariable_pa_k_kernel(tc, x, W, grad_out, out):
             multiply(late[: len(late) // 2])
             quantise_chunk(nc, pools, identity, w_rows[:, 0:ROW_TILES, :], chunk, E4M3_X4, w_codes[0], w_scales[0])
             multiply(late[len(late) // 2 :])
-            late = [(0, c, t) for c in range(chunk[0], chunk[0] + chunk[1]) for t in range(ROW_TILES)]
+            late = [(0, c, t) for t in range(ROW_TILES) for c in range(chunk[0], chunk[0] + chunk[1])]
         for chunk in EVEN_CHUNKS:
             quantise_chunk(nc, pools, identity, w_rows[:, ROW_TILES:EXPERTS, :], chunk, E4M3_X4, w_codes[1], w_scales[1])
-            multiply(late)
-            late = [(1, c, t) for c in range(chunk[0], chunk[0] + chunk[1]) for t in (0, 1)]
+            multiply(late[:RUN_PASSES])
+            select(1)
+            late = late[RUN_PASSES:] + [(1, c, t) for t in (0, 1) for c in range(chunk[0], chunk[0] + chunk[1])]
         multiply(late)
+        select(len(closed))
         for t in (2, 3):
             multiply([(1, c, t) for c in range(PASSES)])
+            select(len(closed))

@@ -33,7 +33,7 @@ RUN_PASSES = 4
 FLOPS = 2 * TOKENS * EXPERTS * D * F
 
 
-def quantise_chunk(nc, pools, identity, rows, chunk, fp8_x4, codes, scales):
+def quantise_chunk(nc, pools, identity, next_bank, after_bank, rows, chunk, fp8_x4, codes, scales):
     first_pass, n_passes = chunk
     grouped = pools["grouped"].tile([P, CHUNK_PASSES, ROW_TILES, P, 4], BF16, name="grouped", align_bytes=64)
     for half in range(ROW_TILES // 2):
@@ -44,7 +44,7 @@ def quantise_chunk(nc, pools, identity, rows, chunk, fp8_x4, codes, scales):
             in_=rows[:, tiles, first_pass * K_PASS : (first_pass + n_passes) * K_PASS],
         )
         for c in range(n_passes):
-            bank = pools["transposed"].tile([P, 2, 2, P], F32, name="bank")
+            bank = next_bank()
             for i in range(2):
                 words = raw[:, i, :].bitcast(F32)
                 for u in range(2):
@@ -55,6 +55,7 @@ def quantise_chunk(nc, pools, identity, rows, chunk, fp8_x4, codes, scales):
                 out=grouped[:, c, tiles, :, :].bitcast(F32),
                 in_=bank[:].rearrange("p i u r -> p i r u"),
             )
+            after_bank()
     for c in range(n_passes):
         nc.vector.quantize_mx(
             out=codes[:, first_pass + c, :].bitcast(fp8_x4),
@@ -75,9 +76,8 @@ def tile_dispatchbyvariable_pa_k_kernel(tc, x, W, grad_out, out):
         pools = {
             "raw": ctx.enter_context(tc.tile_pool(name="raw", bufs=12)),
             "grouped": ctx.enter_context(tc.tile_pool(name="grouped", bufs=3)),
-            "transposed": ctx.enter_context(tc.psum_pool(name="transposed", bufs=4)),
-        }
-        acc_pool = ctx.enter_context(tc.psum_pool(name="acc", bufs=1))
+                    }
+        psum = ctx.enter_context(tc.psum_pool(name="psum", bufs=1))
         ctx.enter_context(tc.manual_schedule())
 
         identity = keep.tile([P, P], F32, name="identity")
@@ -102,13 +102,26 @@ def tile_dispatchbyvariable_pa_k_kernel(tc, x, W, grad_out, out):
         w_codes = [keep.tile([P, PASSES, ROWS], U32, name="w_codes%d" % group, align_bytes=64) for group in range(2)]
         w_scales = [keep.tile([P, PASSES, ROWS], U8, name="w_scales%d" % group, align_bytes=64) for group in range(2)]
         result = keep.tile([P, ROW_TILES, D], F32, name="result")
+        ring = ["bank%d" % n for n in range(4)]
+        fills = {"count": 0}
+        late = []
+
+        def next_bank():
+            return psum.tile([P, 2, 2, P], F32, name=ring[fills["count"] % len(ring)])
+
+        def after_bank():
+            fills["count"] += 1
+            if fills["count"] % len(ring) == 0:
+                multiply(late[: len(ring)])
+                late[: len(ring)] = []
+
         acc = {}
         closed = []
 
         def multiply(todo):
             for group, c, t in todo:
                 if c == 0:
-                    acc[t] = acc_pool.tile([P, ROWS], F32, name="acc%d" % t)
+                    acc[t] = psum.tile([P, ROWS], F32, name="acc%d" % t)
                 tokens = slice(t * P, (t + 1) * P)
                 nc.tensor.matmul_mx(
                     out=acc[t][:],
@@ -123,12 +136,15 @@ def tile_dispatchbyvariable_pa_k_kernel(tc, x, W, grad_out, out):
                     closed.append((group, t))
 
         def select(count):
-            for n in range(min(count, len(closed))):
-                group, t = closed.pop(0)
-                add_selected(group, t)
-
-        def add_selected(group, t):
+            tiles = closed[:count]
+            closed[:] = closed[count:]
             for i in range(ROW_TILES):
+                for group, t in tiles:
+                    add_selected(group, t, i)
+            return tiles
+
+        def add_selected(group, t, i):
+            if True:
                 k = group * ROW_TILES + i
                 if k == 0:
                     nc.vector.tensor_scalar(
@@ -150,18 +166,27 @@ def tile_dispatchbyvariable_pa_k_kernel(tc, x, W, grad_out, out):
             if k == EXPERTS - 1:
                 nc.sync.dma_start(out=out_tiles[t], in_=result[:, t, :])
 
-        late = []
+        fresh = []
         for chunk in TAPERED_CHUNKS:
-            quantise_chunk(nc, pools, identity, g_rows, chunk, E5M2_X4, g_codes, g_scales)
-            multiply(late[: len(late) // 2])
-            quantise_chunk(nc, pools, identity, w_rows[:, 0:ROW_TILES, :], chunk, E4M3_X4, w_codes[0], w_scales[0])
-            multiply(late[len(late) // 2 :])
-            late = [(0, c, t) for t in range(ROW_TILES) for c in range(chunk[0], chunk[0] + chunk[1])]
+            quantise_chunk(nc, pools, identity, next_bank, after_bank, g_rows, chunk, E5M2_X4, g_codes, g_scales)
+            if chunk[1] == 1:
+                multiply(late[: len(late) // 2])
+                late[: len(late) // 2] = []
+            quantise_chunk(nc, pools, identity, next_bank, after_bank, w_rows[:, 0:ROW_TILES, :], chunk, E4M3_X4, w_codes[0], w_scales[0])
+            if chunk[1] == 1:
+                multiply(late)
+                late[:] = []
+                fills["count"] = 0
+            late += [(0, c, t) for t in range(ROW_TILES) for c in range(chunk[0], chunk[0] + chunk[1])]
+        freed = []
         for chunk in EVEN_CHUNKS:
-            quantise_chunk(nc, pools, identity, w_rows[:, ROW_TILES:EXPERTS, :], chunk, E4M3_X4, w_codes[1], w_scales[1])
-            multiply(late[:RUN_PASSES])
-            select(1)
-            late = late[RUN_PASSES:] + [(1, c, t) for t in (0, 1) for c in range(chunk[0], chunk[0] + chunk[1])]
+            quantise_chunk(nc, pools, identity, next_bank, after_bank, w_rows[:, ROW_TILES:EXPERTS, :], chunk, E4M3_X4, w_codes[1], w_scales[1])
+            if len(freed) == 2:
+                ring += freed
+                freed.clear()
+                fills["count"] = 0
+            freed += ["acc%d" % t for group, t in select(2) if t > 1]
+            late += [(1, c, t) for t in (0, 1) for c in range(chunk[0], chunk[0] + chunk[1])]
         multiply(late)
         select(len(closed))
         for t in (2, 3):

from contextlib import ExitStack

import concourse.mybir as mybir
from concourse.masks import make_identity

F32 = mybir.dt.float32
BF16 = mybir.dt.bfloat16
U32 = mybir.dt.uint32
U8 = mybir.dt.uint8
E5M2_X4 = mybir.dt.float8_e5m2_x4
E4M3_X4 = mybir.dt.float8_e4m3fn_x4
ALU = mybir.AluOpType

P = 128
TOKENS = 512
D = 128
F = 8192
EXPERTS = 8
BOUNDARIES = (-1.5, -1.0, -0.5, 0.0, 0.5, 1.0, 1.5)

K_PASS = 4 * P
PASSES = F // K_PASS
WORDS = K_PASS // 2
ROW_TILES = 4
ROWS = ROW_TILES * P

CHUNK_PASSES = 2
EVEN_CHUNKS = [(c, CHUNK_PASSES) for c in range(0, PASSES, CHUNK_PASSES)]
TAPERED_CHUNKS = [(0, 1), (1, 1)] + EVEN_CHUNKS[1:]

RUN_PASSES = 4

FLOPS = 2 * TOKENS * EXPERTS * D * F


def quantise_chunk(nc, pools, identity, next_bank, after_bank, rows, chunk, fp8_x4, codes, scales):
    first_pass, n_passes = chunk
    grouped = pools["grouped"].tile([P, CHUNK_PASSES, ROW_TILES, P, 4], BF16, name="grouped", align_bytes=64)
    for half in range(ROW_TILES // 2):
        tiles = slice(2 * half, 2 * half + 2)
        raw = pools["raw"].tile([P, 2, CHUNK_PASSES * K_PASS], BF16, name="raw")
        nc.sync.dma_start(
            out=raw[:, :, 0 : n_passes * K_PASS],
            in_=rows[:, tiles, first_pass * K_PASS : (first_pass + n_passes) * K_PASS],
        )
        for c in range(n_passes):
            bank = next_bank()
            for i in range(2):
                words = raw[:, i, :].bitcast(F32)
                for u in range(2):
                    start = c * WORDS + u * P
                    nc.tensor.transpose(bank[:, i, u, :], words[:, start : start + P], identity[:])
            copy_out = nc.vector.tensor_copy if (half, c) == (0, 1) else nc.scalar.copy
            copy_out(
                out=grouped[:, c, tiles, :, :].bitcast(F32),
                in_=bank[:].rearrange("p i u r -> p i r u"),
            )
            after_bank()
    for c in range(n_passes):
        nc.vector.quantize_mx(
            out=codes[:, first_pass + c, :].bitcast(fp8_x4),
            scales=scales[:, first_pass + c, :],
            in_=grouped[:, c].rearrange("p t r j -> p (t r j)"),
        )


def tile_dispatchbyvariable_pa_k_kernel(tc, x, W, grad_out, out):
    nc = tc.nc
    x_rows = x.flatten_outer_dims().rearrange("(t p) d -> p t d", p=P)
    g_rows = grad_out.flatten_outer_dims().rearrange("(t p) f -> p t f", p=P)
    w_rows = W.rearrange("k d f -> d k f")
    out_tiles = out.flatten_outer_dims().rearrange("(t p) d -> t p d", p=P)

    with ExitStack() as ctx:
        keep = ctx.enter_context(tc.tile_pool(name="keep", bufs=1))
        pools = {
            "raw": ctx.enter_context(tc.tile_pool(name="raw", bufs=12)),
            "grouped": ctx.enter_context(tc.tile_pool(name="grouped", bufs=3)),
                    }
        psum = ctx.enter_context(tc.psum_pool(name="psum", bufs=1))
        ctx.enter_context(tc.manual_schedule())

        identity = keep.tile([P, P], F32, name="identity")
        make_identity(nc, identity[:])

        x_sb = keep.tile([P, ROW_TILES, D], BF16, name="x_sb")
        nc.scalar.dma_start(out=x_sb[:], in_=x_rows)
        y = keep.tile([P, ROW_TILES], F32, name="y")
        nc.gpsimd.tensor_copy(out=y[:], in_=x_sb[:, :, 0])
        above = keep.tile([P, EXPERTS + 1, ROW_TILES], F32, name="above")
        nc.gpsimd.memset(above[:, 0, :], 1.0)
        nc.gpsimd.memset(above[:, EXPERTS, :], 0.0)
        for j, boundary in enumerate(BOUNDARIES):
            nc.gpsimd.tensor_single_scalar(out=above[:, j + 1, :], in_=y[:], scalar=boundary, op=ALU.is_gt)
        sel = keep.tile([P, EXPERTS, ROW_TILES], F32, name="sel")
        nc.gpsimd.tensor_tensor(
            out=sel[:], in0=above[:, 0:EXPERTS, :], in1=above[:, 1 : EXPERTS + 1, :], op=ALU.subtract
        )

        g_codes = keep.tile([P, PASSES, ROWS], U32, name="g_codes", align_bytes=64)
        g_scales = keep.tile([P, PASSES, ROWS], U8, name="g_scales", align_bytes=64)
        w_codes = [keep.tile([P, PASSES, ROWS], U32, name="w_codes%d" % group, align_bytes=64) for group in range(2)]
        w_scales = [keep.tile([P, PASSES, ROWS], U8, name="w_scales%d" % group, align_bytes=64) for group in range(2)]
        result = keep.tile([P, ROW_TILES, D], F32, name="result")
        ring = ["bank%d" % n for n in range(4)]
        fills = {"count": 0}
        late = []

        def next_bank():
            return psum.tile([P, 2, 2, P], F32, name=ring[fills["count"] % len(ring)])

        def after_bank():
            fills["count"] += 1
            if fills["count"] % len(ring) == 0:
                multiply(late[: len(ring)])
                late[: len(ring)] = []

        acc = {}
        closed = []

        def multiply(todo):
            for group, c, t in todo:
                if c == 0:
                    acc[t] = psum.tile([P, ROWS], F32, name="acc%d" % t)
                tokens = slice(t * P, (t + 1) * P)
                nc.tensor.matmul_mx(
                    out=acc[t][:],
                    lhsT=g_codes[:, c, tokens].bitcast(E5M2_X4),
                    lhsT_scale=g_scales[:, c, tokens],
                    rhs=w_codes[group][:, c, :].bitcast(E4M3_X4),
                    rhs_scale=w_scales[group][:, c, :],
                    start=(c == 0),
                    stop=(c == PASSES - 1),
                )
                if c == PASSES - 1:
                    closed.append((group, t))

        def select(count):
            tiles = closed[:count]
            closed[:] = closed[count:]
            for i in range(ROW_TILES):
                for group, t in tiles:
                    add_selected(group, t, i)
            return tiles

        def add_selected(group, t, i):
            if True:
                k = group * ROW_TILES + i
                if k == 0:
                    nc.vector.tensor_scalar(
                        out=result[:, t, :],
                        in0=acc[t][:, 0:D],
                        scalar1=sel[:, 0, t : t + 1],
                        scalar2=None,
                        op0=ALU.mult,
                    )
                else:
                    nc.vector.scalar_tensor_tensor(
                        out=result[:, t, :],
                        in0=acc[t][:, i * D : (i + 1) * D],
                        scalar=sel[:, k, t : t + 1],
                        in1=result[:, t, :],
                        op0=ALU.mult,
                        op1=ALU.add,
                    )
            if k == EXPERTS - 1:
                nc.sync.dma_start(out=out_tiles[t], in_=result[:, t, :])

        fresh = []
        for chunk in TAPERED_CHUNKS:
            quantise_chunk(nc, pools, identity, next_bank, after_bank, g_rows, chunk, E5M2_X4, g_codes, g_scales)
            if chunk[1] == 1:
                multiply(late[: len(late) // 2])
                late[: len(late) // 2] = []
            quantise_chunk(nc, pools, identity, next_bank, after_bank, w_rows[:, 0:ROW_TILES, :], chunk, E4M3_X4, w_codes[0], w_scales[0])
            if chunk[1] == 1:
                multiply(late)
                late[:] = []
                fills["count"] = 0
            late += [(0, c, t) for t in range(ROW_TILES) for c in range(chunk[0], chunk[0] + chunk[1])]
        freed = []
        for chunk in EVEN_CHUNKS:
            quantise_chunk(nc, pools, identity, next_bank, after_bank, w_rows[:, ROW_TILES:EXPERTS, :], chunk, E4M3_X4, w_codes[1], w_scales[1])
            if len(freed) == 2:
                ring += freed
                freed.clear()
                fills["count"] = 0
            freed += ["acc%d" % t for group, t in select(2) if t > 1]
            late += [(1, c, t) for t in (0, 1) for c in range(chunk[0], chunk[0] + chunk[1])]
        multiply(late)
        select(len(closed))
        for t in (2, 3):
            multiply([(1, c, t) for c in range(PASSES)])
            select(len(closed))
